import numpy as np
import ml_dtypes


def mxq(x, axis, fmt="e4m3"):
    dtype, down = {"e4m3": (ml_dtypes.float8_e4m3fn, 7), "e5m2": (ml_dtypes.float8_e5m2, 14)}[fmt]
    v = np.moveaxis(np.asarray(x, np.float32).astype(ml_dtypes.bfloat16).astype(np.float64), axis, -1)
    blocks = v.reshape(v.shape[:-1] + (-1, 32))
    amax = np.abs(blocks).max(-1, keepdims=True)
    byte = np.maximum(np.where(amax > 0, np.frexp(amax)[1] - 1 + 127, 0) - down, 1)
    scale = np.exp2(byte - 127.0)
    codes = (blocks / scale).astype(np.float32).astype(dtype).astype(np.float64)
    return np.moveaxis((codes * scale).reshape(v.shape), -1, axis)


WIDE = False


def mx_kscale(k):
    if not WIDE:
        return np.ones(k)
    levels = np.array([10, -10, 5, -5, 0])
    if k % 512:
        return np.exp2(np.random.permutation(np.resize(levels, k // 32))).repeat(32)
    a = np.empty((k // 512, 16))
    for p in range(k // 512):
        a[p, :8] = np.random.permutation(np.resize(levels, 8))
        for g in range(8):
            far = levels[np.abs(levels - a[p, g]) >= 10]
            a[p, g + 8] = far[np.random.randint(len(far))]
    return np.exp2(a.ravel()).repeat(32)


BF16 = ml_dtypes.bfloat16


def bf(x):
    return np.asarray(x, np.float32).astype(BF16)


def f64(x):
    return np.asarray(x).astype(np.float64)


B, T, C, H, G, D = 1, 512, 2048, 16, 4, 128
EPS = 1e-6
HALF = D // 2


def rmsnorm(u, w):
    rms = np.sqrt((u * u).sum(-1, keepdims=True)) / np.sqrt(D)
    return w * (u / (rms + EPS))


def rope(u, cos, sin):
    u1, u2 = u[..., :HALF], u[..., HALF:]
    c = cos[None, :, None, :]
    s = sin[None, :, None, :]
    return np.concatenate([u1 * c + u2 * s, -u1 * s + u2 * c], axis=-1)


def draw0():
    s = mx_kscale(C)
    a = 1.0 / np.sqrt(C)
    ang = np.outer(np.arange(T), 1.0 / (10000.0 ** (np.arange(0, D, 2) / D)))
    return {"x": bf(np.random.standard_normal((B, T, C)) * s),
            "Wq": bf(np.random.standard_normal((H * D, C)) * a / s),
            "Wk": bf(np.random.standard_normal((G * D, C)) * a / s),
            "Wv": bf(np.random.standard_normal((G * D, C)) * a / s),
            "q_norm_w": bf(1.0 + 0.1 * np.random.standard_normal(D)),
            "k_norm_w": bf(1.0 + 0.1 * np.random.standard_normal(D)),
            "rope_cos": bf(np.cos(ang)),
            "rope_sin": bf(np.sin(ang))}


def core(x, Wq, Wk, Wv, q_norm_w, k_norm_w, rope_cos, rope_sin):
    xq = mxq(f64(x), 2, "e4m3")
    q = (xq @ mxq(f64(Wq), 1, "e4m3").T).reshape(B, T, H, D)
    k = (xq @ mxq(f64(Wk), 1, "e4m3").T).reshape(B, T, G, D)
    v = (xq @ mxq(f64(Wv), 1, "e4m3").T).reshape(B, T, G, D)
    cos, sin = f64(rope_cos), f64(rope_sin)
    q = rope(rmsnorm(q, f64(q_norm_w)), cos, sin)
    k = rope(rmsnorm(k, f64(k_norm_w)), cos, sin)
    return q, k, v


def e4m3fn_bytes(y):
    return np.clip(np.asarray(y, np.float64), -448.0, 448.0).astype(np.float32).astype(ml_dtypes.float8_e4m3fn).view(np.uint8)


def e4m3fn_values(b):
    return np.asarray(b, np.uint8).view(ml_dtypes.float8_e4m3fn).astype(np.float64)


def setup_inputs():
    d = draw0()
    x0 = np.asarray(d['Wq']).astype(np.float64)
    s = (np.max(np.abs(x0), axis=(0,), keepdims=True) / 448.0).astype(np.float32)
    out = {}
    for k, v in d.items():
        if k == 'Wq':
            out['Wq_bytes'] = e4m3fn_bytes(x0 / s.astype(np.float64))
            out['Wq_scale'] = s
        else:
            out[k] = v
    return out


def reference(x, Wq_bytes, Wq_scale, Wk, Wv, q_norm_w, k_norm_w, rope_cos, rope_sin):
    return core(x, e4m3fn_values(Wq_bytes) * Wq_scale.astype(np.float64), Wk, Wv, q_norm_w, k_norm_w, rope_cos, rope_sin)

@@ -1,0 +1,373 @@
+from contextlib import ExitStack
+
+import concourse.mybir as mybir
+from concourse.masks import make_identity
+
+F32 = mybir.dt.float32
+BF16 = mybir.dt.bfloat16
+U32 = mybir.dt.uint32
+U8 = mybir.dt.uint8
+FP8 = mybir.dt.float8_e4m3fn
+FP8X4 = mybir.dt.float8_e4m3fn_x4
+ALU = mybir.AluOpType
+ACT = mybir.ActivationFunctionType
+
+T, C, H, G, D = 512, 2048, 16, 4, 128
+HALF = D // 2
+EPS = 1e-6
+P = 128
+NG = C // 512
+NT = T // P
+CH = 512
+FLOPS = 2 * T * C * (H + 2 * G) * D
+
+
+def tile_groupedqueryattention_pa_kernel(
+    tc, x, Wq_bytes, Wq_scale, Wk, Wv, q_norm_w, k_norm_w, rope_cos, rope_sin, out_0, out_1, out_2
+):
+    nc = tc.nc
+    x2 = x.flatten_outer_dims()
+    o_q = out_0.rearrange("b t h d -> (b t) (h d)")
+    o_k = out_1.rearrange("b t h d -> (b t) (h d)")
+    o_v = out_2.rearrange("b t h d -> (b t) (h d)")
+
+    with ExitStack() as ctx:
+        const = ctx.enter_context(tc.tile_pool(name="const", bufs=1))
+        rawp = ctx.enter_context(tc.tile_pool(name="rawp", bufs=2))
+        widep = ctx.enter_context(tc.tile_pool(name="widep", bufs=2))
+        grpp = ctx.enter_context(tc.tile_pool(name="grpp", bufs=2))
+        codep = ctx.enter_context(tc.tile_pool(name="codep", bufs=2))
+        prodp = ctx.enter_context(tc.tile_pool(name="prodp", bufs=4))
+        outp = ctx.enter_context(tc.tile_pool(name="outp", bufs=8))
+        statp = ctx.enter_context(tc.tile_pool(name="statp", bufs=3))
+        ptp = ctx.enter_context(tc.psum_pool(name="ptp", bufs=4))
+        accp = ctx.enter_context(tc.psum_pool(name="accp", bufs=4))
+        ctx.enter_context(tc.manual_schedule())
+
+        s_stage = const.tile([P, P], F32, name="s_stage")
+        wq_col = const.tile([P, 1], BF16, name="wq_col")
+        wk_col = const.tile([P, 1], BF16, name="wk_col")
+        cos_t = const.tile([P, NT, HALF], BF16, name="cos_t")
+        sin_t = const.tile([P, NT, HALF], BF16, name="sin_t")
+        nc.gpsimd.memset(s_stage[:], 0.0)
+        nc.scalar.dma_start(out=s_stage[0:16, :], in_=Wq_scale.rearrange("o (m i) -> (o m) i", i=P))
+        nc.sync.dma_start(out=wq_col[:], in_=q_norm_w.rearrange("(p o) -> p o", o=1))
+        nc.sync.dma_start(out=wk_col[:], in_=k_norm_w.rearrange("(p o) -> p o", o=1))
+        nc.scalar.dma_start(out=cos_t[:], in_=rope_cos.rearrange("(a p) j -> p a j", p=P))
+        nc.scalar.dma_start(out=sin_t[:], in_=rope_sin.rearrange("(a p) j -> p a j", p=P))
+
+        qbytes = []
+        for c in range(4):
+            qb = const.tile([P, 4, C], U8, name="qbytes%d" % c)
+            qbytes.append(qb)
+        for rt in range(4):
+            nc.sync.dma_start(out=qbytes[0][:, rt, :], in_=Wq_bytes[P * rt : P * (rt + 1), :])
+
+        def load_bytes(c):
+            nc.sync.dma_start(
+                out=qbytes[c][:],
+                in_=Wq_bytes[CH * c : CH * (c + 1), :].rearrange("(a p) k -> p a k", p=P),
+            )
+
+        def load_rows(dst, src):
+            for rt in range(4):
+                nc.sync.dma_start(out=dst[:, rt, :], in_=src[P * rt : P * (rt + 1), :])
+
+        x_raw = rawp.tile([P, 4, C], BF16, name="x_raw", tag="raw")
+        load_rows(x_raw, x2)
+        load_bytes(1)
+        k_raw = rawp.tile([P, 4, C], BF16, name="k_raw", tag="raw")
+        load_rows(k_raw, Wk)
+        load_bytes(2)
+        load_bytes(3)
+
+        one = const.tile([P, 1], F32, name="one")
+        warm = const.tile([P, 1], F32, name="warm")
+        nc.gpsimd.memset(one[:], 1.0)
+        ident = const.tile([P, P], F32, name="ident")
+        make_identity(nc, ident[:])
+        nc.scalar.activation(out=warm[:], in_=one[:], func=ACT.Sqrt)
+
+        sc = const.tile([P, C], F32, name="sc")
+        s_cols = const.tile([P, 16], F32, name="s_cols")
+        w_cols = const.tile([P, 2], F32, name="w_cols")
+        w_rows = const.tile([P, 2, D], F32, name="w_rows")
+        nc.vector.tensor_copy(out=w_cols[:, 0:1], in_=wq_col[:])
+        nc.vector.tensor_copy(out=w_cols[:, 1:2], in_=wk_col[:])
+        pt = ptp.tile([P, 4, P], F32, name="pt", tag="pt")
+        for j in range(2):
+            nc.tensor.transpose(pt[:, j, :], w_cols[:, j : j + 1].to_broadcast([P, P]), ident[:])
+        nc.scalar.copy(out=w_rows[:], in_=pt[:, 0:2, :])
+        pt = ptp.tile([P, 4, P], F32, name="pt", tag="pt")
+        nc.tensor.transpose(pt[:, 0, :], s_stage[:], ident[:])
+        nc.vector.tensor_copy(out=s_cols[:], in_=pt[:, 0, 0:16])
+        for i in range(4):
+            pt = ptp.tile([P, 4, P], F32, name="pt", tag="pt")
+            for j in range(4):
+                m = 4 * i + j
+                nc.tensor.transpose(pt[:, j, :], s_cols[:, m : m + 1].to_broadcast([P, P]), ident[:])
+            nc.scalar.copy(out=sc[:, 512 * i : 512 * (i + 1)], in_=pt[:].rearrange("p a r -> p (a r)"))
+
+        tabs = {}
+
+        def build_tables(nm, wb):
+            tab = const.tile([P, NT, 2, D], F32, name="tab_" + nm)
+            w1 = wb[:, 0:HALF].unsqueeze(1).to_broadcast([P, NT, HALF])
+            w2 = wb[:, HALF:D].unsqueeze(1).to_broadcast([P, NT, HALF])
+            nc.vector.tensor_tensor(out=tab[:, :, 0, 0:HALF], in0=cos_t[:], in1=w1, op=ALU.mult)
+            nc.vector.tensor_tensor(out=tab[:, :, 0, HALF:D], in0=cos_t[:], in1=w2, op=ALU.mult)
+            return tab, w1, w2
+
+        def build_sin_table(nm, tab, w1, w2):
+            nc.vector.scalar_tensor_tensor(
+                out=tab[:, :, 1, 0:HALF], in0=sin_t[:], scalar=-1.0, in1=w1, op0=ALU.mult, op1=ALU.mult
+            )
+            nc.vector.tensor_tensor(out=tab[:, :, 1, HALF:D], in0=sin_t[:], in1=w2, op=ALU.mult)
+            tabs[nm] = tab
+
+        half_q = build_tables("q", w_rows[:, 0, :])
+        half_k = build_tables("k", w_rows[:, 1, :])
+        build_sin_table("q", *half_q)
+        build_sin_table("k", *half_k)
+
+        x_codes = const.tile([P, NG, T], U32, name="x_codes", align_bytes=64)
+        x_scales = const.tile([P, NG, T], U8, name="x_scales", align_bytes=64)
+        k_codes = const.tile([P, NG, CH], U32, name="k_codes", align_bytes=64)
+        k_scales = const.tile([P, NG, CH], U8, name="k_scales", align_bytes=64)
+        v_codes = const.tile([P, NG, CH], U32, name="v_codes", align_bytes=64)
+        v_scales = const.tile([P, NG, CH], U8, name="v_scales", align_bytes=64)
+        junk = const.tile([P, D], BF16, name="junk")
+
+        def widen(c, rt, wide, cols=slice(0, C)):
+            nc.vector.tensor_tensor(
+                out=wide[:, rt, cols],
+                in0=qbytes[c][:, rt, cols].bitcast(FP8),
+                in1=sc[:, cols],
+                op=ALU.mult,
+            )
+
+        def new_group():
+            grp = grpp.tile([P, NG, 4 * CH], BF16, name="grp", tag="grp", align_bytes=64)
+            return grp
+
+        def turn(rows, rt, grp):
+            words = rows[:, rt, :].bitcast(F32)
+            gwords = grp[:].bitcast(F32)
+            for gp in range(2):
+                pt = ptp.tile([P, 2, 2, P], F32, name="pt", tag="pt")
+                for gg in range(2):
+                    g = 2 * gp + gg
+                    for u in range(2):
+                        nc.tensor.transpose(
+                            pt[:, gg, u, :], words[:, 256 * g + u : 256 * (g + 1) : 2], ident[:]
+                        )
+                nc.scalar.copy(
+                    out=gwords[:, 2 * gp : 2 * gp + 2, 256 * rt : 256 * (rt + 1)].rearrange(
+                        "p g (r u) -> p g r u", u=2
+                    ),
+                    in_=pt[:].rearrange("p g u r -> p g r u"),
+                )
+
+        def quantize_half(grp, codes, scales, gp):
+            gs = slice(2 * gp, 2 * gp + 2)
+            nc.vector.quantize_mx(
+                out=codes[:, gs, :].rearrange("p g n -> p (g n)").bitcast(FP8X4),
+                scales=scales[:, gs, :].rearrange("p g n -> p (g n)"),
+                in_=grp[:, gs, :].rearrange("p g n -> p (g n)"),
+            )
+
+        def quantize(grp, codes, scales):
+            quantize_half(grp, codes, scales, 0)
+            quantize_half(grp, codes, scales, 1)
+
+        def new_codes():
+            codes = codep.tile([P, NG, CH], U32, name="q_codes", tag="q_codes", align_bytes=64)
+            scales = codep.tile([P, NG, CH], U8, name="q_scales", tag="q_scales", align_bytes=64)
+            return codes, scales
+
+        def multiply(codes, scales, pool, tag, tt):
+            acc = pool.tile([P, CH], F32, name="acc", tag=tag)
+            ts = slice(P * tt, P * (tt + 1))
+            for g in range(NG):
+                nc.tensor.matmul_mx(
+                    out=acc[:],
+                    lhsT=x_codes[:, g, ts].bitcast(FP8X4),
+                    lhsT_scale=x_scales[:, g, ts],
+                    rhs=codes[:, g, :].bitcast(FP8X4),
+                    rhs_scale=scales[:, g, :],
+                    start=(g == 0),
+                    stop=(g == NG - 1),
+                )
+            return acc
+
+        def project_normed(codes, scales, pool, tag):
+            ss = statp.tile([P, 16], F32, name="ss", tag="ss")
+            accs = []
+            for tt in range(NT):
+                acc = multiply(codes, scales, pool, tag, tt)
+                for h in range(4):
+                    nc.scalar.activation(
+                        out=junk[:],
+                        in_=acc[:, D * h : D * (h + 1)],
+                        func=ACT.Square,
+                        accum_out=ss[:, 4 * tt + h : 4 * tt + h + 1],
+                    )
+                accs.append(acc)
+            rms = statp.tile([P, 16], F32, name="rms", tag="rms")
+            nc.scalar.activation(out=rms[:], in_=ss[:], func=ACT.Sqrt, scale=1.0 / D)
+            return accs, rms
+
+        def products(accs, nm):
+            prods = []
+            for tt in range(NT):
+                pair = prodp.tile([P, 2, CH], F32, name="pair", tag="pair")
+                nc.vector.tensor_tensor(
+                    out=pair[:].rearrange("p a (h d) -> p a h d", h=4),
+                    in0=accs[tt][:].rearrange("p (h d) -> p h d", h=4).unsqueeze(1).to_broadcast([P, 2, 4, D]),
+                    in1=tabs[nm][:, tt, :, :].unsqueeze(2).to_broadcast([P, 2, 4, D]),
+                    op=ALU.mult,
+                )
+                prods.append(pair)
+            return prods
+
+        def add_eps(rms):
+            den = statp.tile([P, 16], F32, name="den", tag="den")
+            nc.vector.tensor_scalar_add(out=den[:], in0=rms[:], scalar1=EPS)
+            return den
+
+        def invert(den):
+            inv = statp.tile([P, 16], F32, name="inv", tag="inv")
+            nc.vector.reciprocal(out=inv[:], in_=den[:])
+            return inv
+
+        def add_halves(engine, pair, tsum):
+            engine.tensor_tensor(
+                out=tsum[:].rearrange("p (h s j) -> p h s j", s=2, j=HALF),
+                in0=pair[:, 0, :].rearrange("p (h s j) -> p h s j", s=2, j=HALF),
+                in1=pair[:, 1, :].rearrange("p (h s j) -> p h s j", s=2, j=HALF)[:, :, ::-1, :],
+                op=ALU.add,
+            )
+
+        def scale_store(tsum, inv, tt, dst, c, by_vector=False):
+            for h in range(4):
+                hs = slice(D * h, D * (h + 1))
+                factor = inv[:, 4 * tt + h : 4 * tt + h + 1]
+                if by_vector:
+                    nc.vector.tensor_scalar_mul(out=tsum[:, hs], in0=tsum[:, hs], scalar1=factor)
+                else:
+                    nc.scalar.activation(out=tsum[:, hs], in_=tsum[:, hs], func=ACT.Copy, scale=factor)
+            nc.sync.dma_start(out=dst[P * tt : P * (tt + 1), CH * c : CH * (c + 1)], in_=tsum[:])
+
+        def bank(engine, prods, inv, tt, dst, c, by_vector=False):
+            tsum = outp.tile([P, CH], F32, name="tsum", tag="tsum")
+            add_halves(engine, prods[tt], tsum)
+            scale_store(tsum, inv, tt, dst, c, by_vector)
+
+        def held_bank(prods, inv, dst, c):
+            tsum = outp.tile([P, CH], F32, name="tsum", tag="tsum")
+            nc.vector.memset(tsum[:, 0:1], 0.0)
+            add_halves(nc.gpsimd, prods[NT - 1], tsum)
+            scale_store(tsum, inv, NT - 1, dst, c)
+
+        grp_x = new_group()
+        grp_q = new_group()
+        wide = widep.tile([P, 4, C], BF16, name="wide", tag="wide")
+        for g in range(NG):
+            widen(0, 0, wide, slice(512 * g, 512 * (g + 1)))
+        turn(wide, 0, grp_q)
+        turn(x_raw, 0, grp_x)
+        turn(x_raw, 1, grp_x)
+        widen(0, 1, wide)
+        turn(wide, 1, grp_q)
+        turn(x_raw, 2, grp_x)
+        turn(x_raw, 3, grp_x)
+        widen(0, 2, wide)
+        turn(wide, 2, grp_q)
+        widen(0, 3, wide)
+        turn(wide, 3, grp_q)
+        v_raw = rawp.tile([P, 4, C], BF16, name="v_raw", tag="raw")
+        load_rows(v_raw, Wv)
+
+        wide_n = widep.tile([P, 4, C], BF16, name="wide", tag="wide")
+        widen(1, 0, wide_n)
+        widen(1, 1, wide_n)
+        quantize(grp_x, x_codes, x_scales)
+        grp_n = new_group()
+        turn(wide_n, 0, grp_n)
+        turn(wide_n, 1, grp_n)
+        codes, scales = new_codes()
+        quantize(grp_q, codes, scales)
+        accs, rms = project_normed(codes, scales, accp, "acc")
+        widen(1, 2, wide_n)
+        turn(wide_n, 2, grp_n)
+        widen(1, 3, wide_n)
+        turn(wide_n, 3, grp_n)
+
+        held = None
+        for c, side_raw, side_codes, side_scales in (
+            (0, k_raw, k_codes, k_scales),
+            (1, v_raw, None, None),
+        ):
+            grp_s = new_group()
+            for rt in range(4):
+                turn(side_raw, rt, grp_s)
+            if held is not None:
+                held_bank(*held)
+            prods = products(accs, "q")
+            den = add_eps(rms)
+            codes, scales = new_codes()
+            quantize_half(grp_n, codes, scales, 0)
+            inv = invert(den)
+            quantize_half(grp_n, codes, scales, 1)
+            bank(nc.gpsimd, prods, inv, 0, o_q, c)
+            bank(nc.gpsimd, prods, inv, 1, o_q, c)
+            bank(nc.vector, prods, inv, 2, o_q, c)
+            held = (prods, inv, o_q, c)
+            accs, rms = project_normed(codes, scales, accp, "acc")
+            grp_n = new_group()
+            wide_n = widep.tile([P, 4, C], BF16, name="wide", tag="wide")
+            for rt in range(4):
+                widen(c + 2, rt, wide_n)
+                turn(wide_n, rt, grp_n)
+            if side_codes is not None:
+                quantize(grp_s, side_codes, side_scales)
+
+        accs_k, rms_k = project_normed(k_codes, k_scales, ptp, "pt")
+        held_bank(*held)
+        prods = products(accs, "q")
+        den = add_eps(rms)
+        codes, scales = new_codes()
+        quantize_half(grp_n, codes, scales, 0)
+        inv = invert(den)
+        quantize_half(grp_n, codes, scales, 1)
+        den_k = add_eps(rms_k)
+        bank(nc.gpsimd, prods, inv, 0, o_q, 2)
+        bank(nc.gpsimd, prods, inv, 1, o_q, 2)
+        bank(nc.vector, prods, inv, 2, o_q, 2)
+        held = (prods, inv, o_q, 2)
+        accs, rms = project_normed(codes, scales, accp, "acc")
+        quantize_half(grp_s, v_codes, v_scales, 0)
+        inv_k = invert(den_k)
+        quantize_half(grp_s, v_codes, v_scales, 1)
+
+        held_bank(*held)
+        prods = products(accs, "q")
+        den = add_eps(rms)
+        for tt in range(NT):
+            acc = multiply(v_codes, v_scales, accp, "acc", tt)
+            res = outp.tile([P, CH], F32, name="tsum", tag="tsum")
+            nc.scalar.copy(out=res[:], in_=acc[:])
+            nc.sync.dma_start(out=o_v[P * tt : P * (tt + 1), :], in_=res[:])
+        tsum = outp.tile([P, CH], F32, name="tsum", tag="tsum")
+        add_halves(nc.vector, prods[2], tsum)
+        inv = invert(den)
+        bank(nc.gpsimd, prods, inv, 0, o_q, 3)
+        bank(nc.gpsimd, prods, inv, 1, o_q, 3)
+        scale_store(tsum, inv, 2, o_q, 3)
+
+        held_bank(prods, inv, o_q, 3)
+        prods = products(accs_k, "k")
+        bank(nc.gpsimd, prods, inv_k, 0, o_k, 0)
+        bank(nc.gpsimd, prods, inv_k, 1, o_k, 0)
+        bank(nc.vector, prods, inv_k, 2, o_k, 0)
+        bank(nc.vector, prods, inv_k, 3, o_k, 0, by_vector=True)

@@ -217,6 +217,22 @@ def tile_groupedqueryattention_pa_kernel(
             nc.scalar.activation(out=rms[:], in_=ss[:], func=ACT.Sqrt, scale=1.0 / D)
             return accs, rms
 
+        def project_bank(codes, scales, tt, ss):
+            acc = multiply(codes, scales, accp, "acc", tt)
+            for h in range(4):
+                nc.scalar.activation(
+                    out=junk[:],
+                    in_=acc[:, D * h : D * (h + 1)],
+                    func=ACT.Square,
+                    accum_out=ss[:, 4 * tt + h : 4 * tt + h + 1],
+                )
+            return acc
+
+        def root(ss):
+            rms = statp.tile([P, 16], F32, name="rms", tag="rms")
+            nc.scalar.activation(out=rms[:], in_=ss[:], func=ACT.Sqrt, scale=1.0 / D)
+            return rms
+
         def products(accs, nm):
             prods = []
             for tt in range(NT):
@@ -323,12 +339,21 @@ def tile_groupedqueryattention_pa_kernel(
             bank(nc.gpsimd, prods, inv, 1, o_q, c)
             bank(nc.vector, prods, inv, 2, o_q, c)
             held = (prods, inv, o_q, c)
-            accs, rms = project_normed(codes, scales, accp, "acc")
+            ss = statp.tile([P, 16], F32, name="ss", tag="ss")
             grp_n = new_group()
             wide_n = widep.tile([P, 4, C], BF16, name="wide", tag="wide")
-            for rt in range(4):
-                widen(c + 2, rt, wide_n)
-                turn(wide_n, rt, grp_n)
+            accs = [project_bank(codes, scales, 0, ss), project_bank(codes, scales, 1, ss)]
+            widen(c + 2, 0, wide_n)
+            turn(wide_n, 0, grp_n)
+            accs.append(project_bank(codes, scales, 2, ss))
+            widen(c + 2, 1, wide_n)
+            turn(wide_n, 1, grp_n)
+            accs.append(project_bank(codes, scales, 3, ss))
+            rms = root(ss)
+            widen(c + 2, 2, wide_n)
+            turn(wide_n, 2, grp_n)
+            widen(c + 2, 3, wide_n)
+            turn(wide_n, 3, grp_n)
             if side_codes is not None:
                 quantize(grp_s, side_codes, side_scales)
 

@@ -376,23 +376,23 @@ def tile_groupedqueryattention_pa_kernel(
         quantize_half(grp_s, v_codes, v_scales, 1)
 
         held_bank(*held)
-        prods = products(accs, "q")
+        prods = products(accs_k, "k")
         den = add_eps(rms)
         for tt in range(NT):
-            acc = multiply(v_codes, v_scales, accp, "acc", tt)
+            acc = multiply(v_codes, v_scales, ptp, "pt", tt)
             res = outp.tile([P, CH], F32, name="tsum", tag="tsum")
             nc.scalar.copy(out=res[:], in_=acc[:])
             nc.sync.dma_start(out=o_v[P * tt : P * (tt + 1), :], in_=res[:])
         tsum = outp.tile([P, CH], F32, name="tsum", tag="tsum")
         add_halves(nc.vector, prods[2], tsum)
         inv = invert(den)
-        bank(nc.gpsimd, prods, inv, 0, o_q, 3)
-        bank(nc.gpsimd, prods, inv, 1, o_q, 3)
-        scale_store(tsum, inv, 2, o_q, 3)
-
-        held_bank(prods, inv, o_q, 3)
-        prods = products(accs_k, "k")
         bank(nc.gpsimd, prods, inv_k, 0, o_k, 0)
         bank(nc.gpsimd, prods, inv_k, 1, o_k, 0)
-        bank(nc.vector, prods, inv_k, 2, o_k, 0)
-        bank(nc.vector, prods, inv_k, 3, o_k, 0, by_vector=True)
+        scale_store(tsum, inv_k, 2, o_k, 0)
+
+        held_bank(prods, inv_k, o_k, 0)
+        prods = products(accs, "q")
+        bank(nc.gpsimd, prods, inv, 0, o_q, 3)
+        bank(nc.gpsimd, prods, inv, 1, o_q, 3)
+        bank(nc.vector, prods, inv, 2, o_q, 3)
+        bank(nc.vector, prods, inv, 3, o_q, 3, by_vector=True)

@@ -318,6 +318,8 @@ def tile_groupedqueryattention_pa_kernel(
         turn(wide_n, 2, grp_n)
         widen(1, 3, wide_n)
         turn(wide_n, 3, grp_n)
+        wide_a = widep.tile([P, 4, C], BF16, name="wide", tag="wide")
+        widen(2, 0, wide_a)
 
         held = None
         for c, side_raw, side_codes, side_scales in (
@@ -341,21 +343,22 @@ def tile_groupedqueryattention_pa_kernel(
             held = (prods, inv, o_q, c)
             ss = statp.tile([P, 16], F32, name="ss", tag="ss")
             grp_n = new_group()
-            wide_n = widep.tile([P, 4, C], BF16, name="wide", tag="wide")
-            accs = [project_bank(codes, scales, 0, ss), project_bank(codes, scales, 1, ss)]
-            widen(c + 2, 0, wide_n)
+            wide_n = wide_a
             turn(wide_n, 0, grp_n)
-            accs.append(project_bank(codes, scales, 2, ss))
+            accs = [project_bank(codes, scales, 0, ss), project_bank(codes, scales, 1, ss)]
             widen(c + 2, 1, wide_n)
             turn(wide_n, 1, grp_n)
-            accs.append(project_bank(codes, scales, 3, ss))
-            rms = root(ss)
+            accs.append(project_bank(codes, scales, 2, ss))
             widen(c + 2, 2, wide_n)
             turn(wide_n, 2, grp_n)
+            accs.append(project_bank(codes, scales, 3, ss))
+            rms = root(ss)
             widen(c + 2, 3, wide_n)
             turn(wide_n, 3, grp_n)
             if side_codes is not None:
                 quantize(grp_s, side_codes, side_scales)
+                wide_a = widep.tile([P, 4, C], BF16, name="wide", tag="wide")
+                widen(3, 0, wide_a)
 
         accs_k, rms_k = project_normed(k_codes, k_scales, ptp, "pt")
         held_bank(*held)

@@ -45,16 +45,16 @@ def tile_groupedqueryattention_pa_kernel(
         ctx.enter_context(tc.manual_schedule())
 
         s_stage = const.tile([P, P], F32, name="s_stage")
-        wq_col = const.tile([P, 1], BF16, name="wq_col")
-        wk_col = const.tile([P, 1], BF16, name="wk_col")
-        cos_t = const.tile([P, NT, HALF], BF16, name="cos_t")
-        sin_t = const.tile([P, NT, HALF], BF16, name="sin_t")
+        g_stage = const.tile([P, 2, D], BF16, name="g_stage")
+        cs = const.tile([P, NT, 2, HALF], BF16, name="cs")
         nc.gpsimd.memset(s_stage[:], 0.0)
-        nc.scalar.dma_start(out=s_stage[0:16, :], in_=Wq_scale.rearrange("o (m i) -> (o m) i", i=P))
-        nc.sync.dma_start(out=wq_col[:], in_=q_norm_w.rearrange("(p o) -> p o", o=1))
-        nc.sync.dma_start(out=wk_col[:], in_=k_norm_w.rearrange("(p o) -> p o", o=1))
-        nc.scalar.dma_start(out=cos_t[:], in_=rope_cos.rearrange("(a p) j -> p a j", p=P))
-        nc.scalar.dma_start(out=sin_t[:], in_=rope_sin.rearrange("(a p) j -> p a j", p=P))
+        nc.vector.memset(g_stage[:], 0.0)
+        nc.sync.dma_start(out=s_stage[0:16, :], in_=Wq_scale.rearrange("o (m i) -> (o m) i", i=P))
+        for row, w in ((0, q_norm_w), (1, k_norm_w)):
+            nc.scalar.dma_start(
+                out=g_stage[row : row + 1, :, :],
+                in_=w.rearrange("(o d) -> o d", o=1).unsqueeze(1).to_broadcast([1, 2, D]),
+            )
 
         qbytes = []
         for c in range(4):
@@ -62,6 +62,8 @@ def tile_groupedqueryattention_pa_kernel(
             qbytes.append(qb)
         for rt in range(4):
             nc.sync.dma_start(out=qbytes[0][:, rt, :], in_=Wq_bytes[P * rt : P * (rt + 1), :])
+        nc.sync.dma_start(out=cs[:, :, 0, :], in_=rope_cos.rearrange("(a p) j -> p a j", p=P))
+        nc.sync.dma_start(out=cs[:, :, 1, :], in_=rope_sin.rearrange("(a p) j -> p a j", p=P))
 
         def load_bytes(c):
             nc.sync.dma_start(
@@ -90,14 +92,6 @@ def tile_groupedqueryattention_pa_kernel(
 
         sc = const.tile([P, C], F32, name="sc")
         s_cols = const.tile([P, 16], F32, name="s_cols")
-        w_cols = const.tile([P, 2], F32, name="w_cols")
-        w_rows = const.tile([P, 2, D], F32, name="w_rows")
-        nc.vector.tensor_copy(out=w_cols[:, 0:1], in_=wq_col[:])
-        nc.vector.tensor_copy(out=w_cols[:, 1:2], in_=wk_col[:])
-        pt = ptp.tile([P, 4, P], F32, name="pt", tag="pt")
-        for j in range(2):
-            nc.tensor.transpose(pt[:, j, :], w_cols[:, j : j + 1].to_broadcast([P, P]), ident[:])
-        nc.scalar.copy(out=w_rows[:], in_=pt[:, 0:2, :])
         pt = ptp.tile([P, 4, P], F32, name="pt", tag="pt")
         nc.tensor.transpose(pt[:, 0, :], s_stage[:], ident[:])
         nc.vector.tensor_copy(out=s_cols[:], in_=pt[:, 0, 0:16])
@@ -108,27 +102,56 @@ def tile_groupedqueryattention_pa_kernel(
                 nc.tensor.transpose(pt[:, j, :], s_cols[:, m : m + 1].to_broadcast([P, P]), ident[:])
             nc.scalar.copy(out=sc[:, 512 * i : 512 * (i + 1)], in_=pt[:].rearrange("p a r -> p (a r)"))
 
-        tabs = {}
+        ident_b = const.tile([P, P], BF16, name="ident_b")
+        make_identity(nc, ident_b[:])
+        g_cols = const.tile([P, 2, 2], F32, name="g_cols")
+        g_neg = const.tile([P, 2], F32, name="g_neg")
+        cs_t = const.tile([P, NT, P], BF16, name="cs_t")
+        diag = const.tile([P, 2, 4, HALF], BF16, name="diag")
+        tab_q = const.tile([P, NT, 2, D], F32, name="tab_q")
+        tab_k = const.tile([P, NT, 2, D], F32, name="tab_k")
+        tabs = {"q": tab_q, "k": tab_k}
 
-        def build_tables(nm, wb):
-            tab = const.tile([P, NT, 2, D], F32, name="tab_" + nm)
-            w1 = wb[:, 0:HALF].unsqueeze(1).to_broadcast([P, NT, HALF])
-            w2 = wb[:, HALF:D].unsqueeze(1).to_broadcast([P, NT, HALF])
-            nc.vector.tensor_tensor(out=tab[:, :, 0, 0:HALF], in0=cos_t[:], in1=w1, op=ALU.mult)
-            nc.vector.tensor_tensor(out=tab[:, :, 0, HALF:D], in0=cos_t[:], in1=w2, op=ALU.mult)
-            return tab, w1, w2
+        def tables_turn():
+            ptb = ptp.tile([P, NT + 2, P], BF16, name="pt", tag="pt")
+            twice = g_stage[:].rearrange("p r d -> p (r d)")
+            nc.tensor.transpose(ptb[:, NT, :], twice[:, 0:D], ident_b[:])
+            nc.tensor.transpose(ptb[:, NT + 1, :], twice[:, HALF : HALF + D], ident_b[:])
+            for a in range(NT):
+                nc.tensor.transpose(ptb[:, a, :], cs[:, a, :, :].rearrange("p s j -> p (s j)"), ident_b[:])
+            nc.scalar.copy(out=g_cols[:], in_=ptb[:, NT : NT + 2, 0:2])
+            nc.scalar.activation(out=g_neg[:], in_=ptb[:, NT + 1, 0:2], func=ACT.Copy, scale=-1.0)
+            nc.scalar.copy(out=cs_t[:], in_=ptb[:, 0:NT, :])
+            for n in range(2):
+                nc.scalar.activation(
+                    out=diag[:, n, 0::3, :],
+                    in_=ident[:].rearrange("p (b j) -> p b j", b=2),
+                    func=ACT.Copy,
+                    scale=g_cols[:, 0, n : n + 1],
+                )
+                nc.scalar.activation(
+                    out=diag[:, n, 1, :], in_=ident[:, 0:HALF], func=ACT.Copy, scale=g_cols[:, 1, n : n + 1]
+                )
+                nc.scalar.activation(
+                    out=diag[:, n, 2, :], in_=ident[:, HALF:P], func=ACT.Copy, scale=g_neg[:, n : n + 1]
+                )
 
-        def build_sin_table(nm, tab, w1, w2):
-            nc.vector.scalar_tensor_tensor(
-                out=tab[:, :, 1, 0:HALF], in0=sin_t[:], scalar=-1.0, in1=w1, op0=ALU.mult, op1=ALU.mult
-            )
-            nc.vector.tensor_tensor(out=tab[:, :, 1, HALF:D], in0=sin_t[:], in1=w2, op=ALU.mult)
-            tabs[nm] = tab
-
-        half_q = build_tables("q", w_rows[:, 0, :])
-        half_k = build_tables("k", w_rows[:, 1, :])
-        build_sin_table("q", *half_q)
-        build_sin_table("k", *half_k)
+        def tables_multiply():
+            for n, nm in enumerate(("q", "k")):
+                for i in range(2):
+                    ptab = ptp.tile([P, 2, 2 * D], F32, name="pt", tag="pt")
+                    for j in range(2):
+                        nc.tensor.matmul(
+                            out=ptab[:, j, :],
+                            lhsT=cs_t[:, 2 * i + j, :],
+                            rhs=diag[:, n, :, :].rearrange("p b j -> p (b j)"),
+                            start=True,
+                            stop=True,
+                        )
+                    nc.scalar.copy(
+                        out=tabs[nm][:, 2 * i : 2 * i + 2, :, :].rearrange("p a s d -> p (a s d)"),
+                        in_=ptab[:].rearrange("p a n -> p (a n)"),
+                    )
 
         x_codes = const.tile([P, NG, T], U32, name="x_codes", align_bytes=64)
         x_scales = const.tile([P, NG, T], U8, name="x_scales", align_bytes=64)
@@ -151,9 +174,13 @@ def tile_groupedqueryattention_pa_kernel(
             return grp
 
         def turn(rows, rt, grp):
+            turn_half(rows, rt, grp, 0)
+            turn_half(rows, rt, grp, 1)
+
+        def turn_half(rows, rt, grp, half):
             words = rows[:, rt, :].bitcast(F32)
             gwords = grp[:].bitcast(F32)
-            for gp in range(2):
+            for gp in (half,):
                 pt = ptp.tile([P, 2, 2, P], F32, name="pt", tag="pt")
                 for gg in range(2):
                     g = 2 * gp + gg
@@ -215,7 +242,7 @@ def tile_groupedqueryattention_pa_kernel(
                 accs.append(acc)
             rms = statp.tile([P, 16], F32, name="rms", tag="rms")
             nc.scalar.activation(out=rms[:], in_=ss[:], func=ACT.Sqrt, scale=1.0 / D)
-            return accs, rms
+            return accs, plus_eps(rms)
 
         def project_bank(codes, scales, tt, ss):
             acc = multiply(codes, scales, accp, "acc", tt)
@@ -231,7 +258,7 @@ def tile_groupedqueryattention_pa_kernel(
         def root(ss):
             rms = statp.tile([P, 16], F32, name="rms", tag="rms")
             nc.scalar.activation(out=rms[:], in_=ss[:], func=ACT.Sqrt, scale=1.0 / D)
-            return rms
+            return plus_eps(rms)
 
         def products(accs, nm):
             prods = []
@@ -246,9 +273,12 @@ def tile_groupedqueryattention_pa_kernel(
                 prods.append(pair)
             return prods
 
-        def add_eps(rms):
+        def plus_eps(rms):
             den = statp.tile([P, 16], F32, name="den", tag="den")
-            nc.vector.tensor_scalar_add(out=den[:], in0=rms[:], scalar1=EPS)
+            nc.scalar.activation(out=den[:], in_=rms[:], func=ACT.Copy, bias=EPS)
+            return den
+
+        def add_eps(den):
             return den
 
         def invert(den):
@@ -256,9 +286,20 @@ def tile_groupedqueryattention_pa_kernel(
             nc.vector.reciprocal(out=inv[:], in_=den[:])
             return inv
 
+        spare = []
+        taken = [0]
+
+        def new_out():
+            if taken[0] < len(spare):
+                place = spare[taken[0]]
+                taken[0] = taken[0] + 1
+                return place
+            tile = outp.tile([P, CH], F32, name="tsum", tag="tsum")
+            return tile[:]
+
         def add_halves(engine, pair, tsum):
             engine.tensor_tensor(
-                out=tsum[:].rearrange("p (h s j) -> p h s j", s=2, j=HALF),
+                out=tsum.rearrange("p (h s j) -> p h s j", s=2, j=HALF),
                 in0=pair[:, 0, :].rearrange("p (h s j) -> p h s j", s=2, j=HALF),
                 in1=pair[:, 1, :].rearrange("p (h s j) -> p h s j", s=2, j=HALF)[:, :, ::-1, :],
                 op=ALU.add,
@@ -272,15 +313,15 @@ def tile_groupedqueryattention_pa_kernel(
                     nc.vector.tensor_scalar_mul(out=tsum[:, hs], in0=tsum[:, hs], scalar1=factor)
                 else:
                     nc.scalar.activation(out=tsum[:, hs], in_=tsum[:, hs], func=ACT.Copy, scale=factor)
-            nc.sync.dma_start(out=dst[P * tt : P * (tt + 1), CH * c : CH * (c + 1)], in_=tsum[:])
+            nc.sync.dma_start(out=dst[P * tt : P * (tt + 1), CH * c : CH * (c + 1)], in_=tsum)
 
         def bank(engine, prods, inv, tt, dst, c, by_vector=False):
-            tsum = outp.tile([P, CH], F32, name="tsum", tag="tsum")
+            tsum = new_out()
             add_halves(engine, prods[tt], tsum)
             scale_store(tsum, inv, tt, dst, c, by_vector)
 
         def held_bank(prods, inv, dst, c):
-            tsum = outp.tile([P, CH], F32, name="tsum", tag="tsum")
+            tsum = new_out()
             nc.vector.memset(tsum[:, 0:1], 0.0)
             add_halves(nc.gpsimd, prods[NT - 1], tsum)
             scale_store(tsum, inv, NT - 1, dst, c)
@@ -289,18 +330,15 @@ def tile_groupedqueryattention_pa_kernel(
         grp_q = new_group()
         wide = widep.tile([P, 4, C], BF16, name="wide", tag="wide")
         for g in range(NG):
-            widen(0, 0, wide, slice(512 * g, 512 * (g + 1)))
-        turn(wide, 0, grp_q)
-        turn(x_raw, 0, grp_x)
-        turn(x_raw, 1, grp_x)
-        widen(0, 1, wide)
-        turn(wide, 1, grp_q)
-        turn(x_raw, 2, grp_x)
-        turn(x_raw, 3, grp_x)
-        widen(0, 2, wide)
-        turn(wide, 2, grp_q)
-        widen(0, 3, wide)
-        turn(wide, 3, grp_q)
+            for rt in range(4):
+                widen(0, rt, wide, slice(512 * g, 512 * (g + 1)))
+            if g % 2 == 0:
+                turn(x_raw, g, grp_x)
+                turn(x_raw, g + 1, grp_x)
+            else:
+                for rt in range(4):
+                    turn_half(wide, rt, grp_q, g // 2)
+        tables_turn()
         v_raw = rawp.tile([P, 4, C], BF16, name="v_raw", tag="raw")
         load_rows(v_raw, Wv)
 
@@ -311,6 +349,7 @@ def tile_groupedqueryattention_pa_kernel(
         grp_n = new_group()
         turn(wide_n, 0, grp_n)
         turn(wide_n, 1, grp_n)
+        tables_multiply()
         codes, scales = new_codes()
         quantize(grp_q, codes, scales)
         accs, rms = project_normed(codes, scales, accp, "acc")
@@ -360,6 +399,9 @@ def tile_groupedqueryattention_pa_kernel(
                 wide_a = widep.tile([P, 4, C], BF16, name="wide", tag="wide")
                 widen(3, 0, wide_a)
 
+        for i in range(2):
+            big = widep.tile([P, 8, CH], F32, name="wide", tag="wide")
+            spare.extend([big[:, j, :] for j in range(8)])
         accs_k, rms_k = project_normed(k_codes, k_scales, ptp, "pt")
         held_bank(*held)
         prods = products(accs, "q")
@@ -383,10 +425,10 @@ def tile_groupedqueryattention_pa_kernel(
         den = add_eps(rms)
         for tt in range(NT):
             acc = multiply(v_codes, v_scales, ptp, "pt", tt)
-            res = outp.tile([P, CH], F32, name="tsum", tag="tsum")
-            nc.scalar.copy(out=res[:], in_=acc[:])
-            nc.sync.dma_start(out=o_v[P * tt : P * (tt + 1), :], in_=res[:])
-        tsum = outp.tile([P, CH], F32, name="tsum", tag="tsum")
+            res = new_out()
+            nc.scalar.copy(out=res, in_=acc[:])
+            nc.sync.dma_start(out=o_v[P * tt : P * (tt + 1), :], in_=res)
+        tsum = new_out()
         add_halves(nc.vector, prods[2], tsum)
         inv = invert(den)
         bank(nc.gpsimd, prods, inv_k, 0, o_k, 0)

@@ -159,7 +159,16 @@ def tile_groupedqueryattention_pa_kernel(
         k_scales = const.tile([P, NG, CH], U8, name="k_scales", align_bytes=64)
         v_codes = const.tile([P, NG, CH], U32, name="v_codes", align_bytes=64)
         v_scales = const.tile([P, NG, CH], U8, name="v_scales", align_bytes=64)
-        junk = const.tile([P, D], BF16, name="junk")
+        junks = []
+        for i in range(8):
+            junk_tile = const.tile([P, D], BF16, name="junk%d" % i)
+            junks.append(junk_tile)
+        turn_of_junk = [0]
+
+        def junk():
+            turn_of_junk[0] = (turn_of_junk[0] + 1) % 8
+            return junks[turn_of_junk[0]][:]
+
 
         def widen(c, rt, wide, cols=slice(0, C)):
             nc.vector.tensor_tensor(
@@ -234,7 +243,7 @@ def tile_groupedqueryattention_pa_kernel(
                 acc = multiply(codes, scales, pool, tag, tt)
                 for h in range(4):
                     nc.scalar.activation(
-                        out=junk[:],
+                        out=junk(),
                         in_=acc[:, D * h : D * (h + 1)],
                         func=ACT.Square,
                         accum_out=ss[:, 4 * tt + h : 4 * tt + h + 1],
@@ -248,7 +257,7 @@ def tile_groupedqueryattention_pa_kernel(
             acc = multiply(codes, scales, accp, "acc", tt)
             for h in range(4):
                 nc.scalar.activation(
-                    out=junk[:],
+                    out=junk(),
                     in_=acc[:, D * h : D * (h + 1)],
                     func=ACT.Square,
                     accum_out=ss[:, 4 * tt + h : 4 * tt + h + 1],

@@ -95,12 +95,13 @@ def tile_groupedqueryattention_pa_kernel(
         pt = ptp.tile([P, 4, P], F32, name="pt", tag="pt")
         nc.tensor.transpose(pt[:, 0, :], s_stage[:], ident[:])
         nc.vector.tensor_copy(out=s_cols[:], in_=pt[:, 0, 0:16])
-        for i in range(4):
+        for first, last in ((0, 2), (2, 6), (6, 10), (10, 14), (14, 16)):
+            n = last - first
             pt = ptp.tile([P, 4, P], F32, name="pt", tag="pt")
-            for j in range(4):
-                m = 4 * i + j
+            for j in range(n):
+                m = first + j
                 nc.tensor.transpose(pt[:, j, :], s_cols[:, m : m + 1].to_broadcast([P, P]), ident[:])
-            nc.scalar.copy(out=sc[:, 512 * i : 512 * (i + 1)], in_=pt[:].rearrange("p a r -> p (a r)"))
+            nc.scalar.copy(out=sc[:, P * first : P * last], in_=pt[:, 0:n, :].rearrange("p a r -> p (a r)"))
 
         ident_b = const.tile([P, P], BF16, name="ident_b")
         make_identity(nc, ident_b[:])
@@ -338,15 +339,12 @@ def tile_groupedqueryattention_pa_kernel(
         grp_x = new_group()
         grp_q = new_group()
         wide = widep.tile([P, 4, C], BF16, name="wide", tag="wide")
-        for g in range(NG):
+        for first, last in ((0, 256), (256, 768), (768, 2048)):
             for rt in range(4):
-                widen(0, rt, wide, slice(512 * g, 512 * (g + 1)))
-            if g % 2 == 0:
-                turn(x_raw, g, grp_x)
-                turn(x_raw, g + 1, grp_x)
-            else:
-                for rt in range(4):
-                    turn_half(wide, rt, grp_q, g // 2)
+                widen(0, rt, wide, slice(first, last))
+                if last == C:
+                    turn(x_raw, rt, grp_x)
+                    turn(wide, rt, grp_q)
         tables_turn()
         v_raw = rawp.tile([P, 4, C], BF16, name="v_raw", tag="raw")
         load_rows(v_raw, Wv)

@@ -430,21 +430,27 @@ def tile_groupedqueryattention_pa_kernel(
         held_bank(*held)
         prods = products(accs_k, "k")
         den = add_eps(rms)
-        for tt in range(NT):
+
+        def finish_v(tt):
             acc = multiply(v_codes, v_scales, ptp, "pt", tt)
             res = new_out()
             nc.scalar.copy(out=res, in_=acc[:])
             nc.sync.dma_start(out=o_v[P * tt : P * (tt + 1), :], in_=res)
+
+        finish_v(0)
+        bank(nc.gpsimd, prods, inv_k, 0, o_k, 0)
+        finish_v(1)
+        bank(nc.gpsimd, prods, inv_k, 1, o_k, 0)
+        finish_v(2)
         tsum = new_out()
         add_halves(nc.vector, prods[2], tsum)
         inv = invert(den)
-        bank(nc.gpsimd, prods, inv_k, 0, o_k, 0)
-        bank(nc.gpsimd, prods, inv_k, 1, o_k, 0)
         scale_store(tsum, inv_k, 2, o_k, 0)
+        finish_v(3)
 
         held_bank(prods, inv_k, o_k, 0)
         prods = products(accs, "q")
         bank(nc.gpsimd, prods, inv, 0, o_q, 3)
         bank(nc.gpsimd, prods, inv, 1, o_q, 3)
-        bank(nc.vector, prods, inv, 2, o_q, 3)
+        bank(nc.vector, prods, inv, 2, o_q, 3, by_vector=True)
         bank(nc.vector, prods, inv, 3, o_q, 3, by_vector=True)

from contextlib import ExitStack

import concourse.mybir as mybir
from concourse.masks import make_identity

F32 = mybir.dt.float32
BF16 = mybir.dt.bfloat16
U32 = mybir.dt.uint32
U8 = mybir.dt.uint8
FP8 = mybir.dt.float8_e4m3fn
FP8X4 = mybir.dt.float8_e4m3fn_x4
ALU = mybir.AluOpType
ACT = mybir.ActivationFunctionType

T, C, H, G, D = 512, 2048, 16, 4, 128
HALF = D // 2
EPS = 1e-6
P = 128
NG = C // 512
NT = T // P
CH = 512
FLOPS = 2 * T * C * (H + 2 * G) * D


def tile_groupedqueryattention_pa_kernel(
    tc, x, Wq_bytes, Wq_scale, Wk, Wv, q_norm_w, k_norm_w, rope_cos, rope_sin, out_0, out_1, out_2
):
    nc = tc.nc
    x2 = x.flatten_outer_dims()
    o_q = out_0.rearrange("b t h d -> (b t) (h d)")
    o_k = out_1.rearrange("b t h d -> (b t) (h d)")
    o_v = out_2.rearrange("b t h d -> (b t) (h d)")

    with ExitStack() as ctx:
        const = ctx.enter_context(tc.tile_pool(name="const", bufs=1))
        rawp = ctx.enter_context(tc.tile_pool(name="rawp", bufs=2))
        widep = ctx.enter_context(tc.tile_pool(name="widep", bufs=2))
        grpp = ctx.enter_context(tc.tile_pool(name="grpp", bufs=2))
        codep = ctx.enter_context(tc.tile_pool(name="codep", bufs=2))
        prodp = ctx.enter_context(tc.tile_pool(name="prodp", bufs=4))
        outp = ctx.enter_context(tc.tile_pool(name="outp", bufs=8))
        statp = ctx.enter_context(tc.tile_pool(name="statp", bufs=3))
        ptp = ctx.enter_context(tc.psum_pool(name="ptp", bufs=4))
        accp = ctx.enter_context(tc.psum_pool(name="accp", bufs=4))
        ctx.enter_context(tc.manual_schedule())

        s_stage = const.tile([P, P], F32, name="s_stage")
        g_stage = const.tile([P, 2, D], BF16, name="g_stage")
        cs = const.tile([P, NT, 2, HALF], BF16, name="cs")
        nc.gpsimd.memset(s_stage[:], 0.0)
        nc.vector.memset(g_stage[:], 0.0)
        nc.sync.dma_start(out=s_stage[0:16, :], in_=Wq_scale.rearrange("o (m i) -> (o m) i", i=P))
        for row, w in ((0, q_norm_w), (1, k_norm_w)):
            nc.scalar.dma_start(
                out=g_stage[row : row + 1, :, :],
                in_=w.rearrange("(o d) -> o d", o=1).unsqueeze(1).to_broadcast([1, 2, D]),
            )

        qbytes = []
        for c in range(4):
            qb = const.tile([P, 4, C], U8, name="qbytes%d" % c)
            qbytes.append(qb)
        for rt in range(4):
            nc.sync.dma_start(out=qbytes[0][:, rt, :], in_=Wq_bytes[P * rt : P * (rt + 1), :])
        nc.sync.dma_start(out=cs[:, :, 0, :], in_=rope_cos.rearrange("(a p) j -> p a j", p=P))
        nc.sync.dma_start(out=cs[:, :, 1, :], in_=rope_sin.rearrange("(a p) j -> p a j", p=P))

        def load_bytes(c):
            nc.sync.dma_start(
                out=qbytes[c][:],
                in_=Wq_bytes[CH * c : CH * (c + 1), :].rearrange("(a p) k -> p a k", p=P),
            )

        def load_rows(dst, src):
            for rt in range(4):
                nc.sync.dma_start(out=dst[:, rt, :], in_=src[P * rt : P * (rt + 1), :])

        x_raw = rawp.tile([P, 4, C], BF16, name="x_raw", tag="raw")
        load_rows(x_raw, x2)
        load_bytes(1)
        k_raw = rawp.tile([P, 4, C], BF16, name="k_raw", tag="raw")
        load_rows(k_raw, Wk)
        load_bytes(2)
        load_bytes(3)

        one = const.tile([P, 1], F32, name="one")
        warm = const.tile([P, 1], F32, name="warm")
        nc.gpsimd.memset(one[:], 1.0)
        ident = const.tile([P, P], F32, name="ident")
        make_identity(nc, ident[:])
        nc.scalar.activation(out=warm[:], in_=one[:], func=ACT.Sqrt)

        sc = const.tile([P, C], F32, name="sc")
        s_cols = const.tile([P, 16], F32, name="s_cols")
        pt = ptp.tile([P, 4, P], F32, name="pt", tag="pt")
        nc.tensor.transpose(pt[:, 0, :], s_stage[:], ident[:])
        nc.vector.tensor_copy(out=s_cols[:], in_=pt[:, 0, 0:16])
        for first, last in ((0, 2), (2, 6), (6, 10), (10, 14), (14, 16)):
            n = last - first
            pt = ptp.tile([P, 4, P], F32, name="pt", tag="pt")
            for j in range(n):
                m = first + j
                nc.tensor.transpose(pt[:, j, :], s_cols[:, m : m + 1].to_broadcast([P, P]), ident[:])
            nc.scalar.copy(out=sc[:, P * first : P * last], in_=pt[:, 0:n, :].rearrange("p a r -> p (a r)"))

        ident_b = const.tile([P, P], BF16, name="ident_b")
        make_identity(nc, ident_b[:])
        g_cols = const.tile([P, 2, 2], F32, name="g_cols")
        g_neg = const.tile([P, 2], F32, name="g_neg")
        cs_t = const.tile([P, NT, P], BF16, name="cs_t")
        diag = const.tile([P, 2, 4, HALF], BF16, name="diag")
        tab_q = const.tile([P, NT, 2, D], F32, name="tab_q")
        tab_k = const.tile([P, NT, 2, D], F32, name="tab_k")
        tabs = {"q": tab_q, "k": tab_k}

        def tables_turn():
            ptb = ptp.tile([P, NT + 2, P], BF16, name="pt", tag="pt")
            twice = g_stage[:].rearrange("p r d -> p (r d)")
            nc.tensor.transpose(ptb[:, NT, :], twice[:, 0:D], ident_b[:])
            nc.tensor.transpose(ptb[:, NT + 1, :], twice[:, HALF : HALF + D], ident_b[:])
            for a in range(NT):
                nc.tensor.transpose(ptb[:, a, :], cs[:, a, :, :].rearrange("p s j -> p (s j)"), ident_b[:])
            nc.scalar.copy(out=g_cols[:], in_=ptb[:, NT : NT + 2, 0:2])
            nc.scalar.activation(out=g_neg[:], in_=ptb[:, NT + 1, 0:2], func=ACT.Copy, scale=-1.0)
            nc.scalar.copy(out=cs_t[:], in_=ptb[:, 0:NT, :])
            for n in range(2):
                nc.scalar.activation(
                    out=diag[:, n, 0::3, :],
                    in_=ident[:].rearrange("p (b j) -> p b j", b=2),
                    func=ACT.Copy,
                    scale=g_cols[:, 0, n : n + 1],
                )
                nc.scalar.activation(
                    out=diag[:, n, 1, :], in_=ident[:, 0:HALF], func=ACT.Copy, scale=g_cols[:, 1, n : n + 1]
                )
                nc.scalar.activation(
                    out=diag[:, n, 2, :], in_=ident[:, HALF:P], func=ACT.Copy, scale=g_neg[:, n : n + 1]
                )

        def tables_multiply():
            for n, nm in enumerate(("q", "k")):
                for i in range(2):
                    ptab = ptp.tile([P, 2, 2 * D], F32, name="pt", tag="pt")
                    for j in range(2):
                        nc.tensor.matmul(
                            out=ptab[:, j, :],
                            lhsT=cs_t[:, 2 * i + j, :],
                            rhs=diag[:, n, :, :].rearrange("p b j -> p (b j)"),
                            start=True,
                            stop=True,
                        )
                    nc.scalar.copy(
                        out=tabs[nm][:, 2 * i : 2 * i + 2, :, :].rearrange("p a s d -> p (a s d)"),
                        in_=ptab[:].rearrange("p a n -> p (a n)"),
                    )

        x_codes = const.tile([P, NG, T], U32, name="x_codes", align_bytes=64)
        x_scales = const.tile([P, NG, T], U8, name="x_scales", align_bytes=64)
        k_codes = const.tile([P, NG, CH], U32, name="k_codes", align_bytes=64)
        k_scales = const.tile([P, NG, CH], U8, name="k_scales", align_bytes=64)
        v_codes = const.tile([P, NG, CH], U32, name="v_codes", align_bytes=64)
        v_scales = const.tile([P, NG, CH], U8, name="v_scales", align_bytes=64)
        junks = []
        for i in range(8):
            junk_tile = const.tile([P, D], BF16, name="junk%d" % i)
            junks.append(junk_tile)
        turn_of_junk = [0]

        def junk():
            turn_of_junk[0] = (turn_of_junk[0] + 1) % 8
            return junks[turn_of_junk[0]][:]


        def widen(c, rt, wide, cols=slice(0, C)):
            nc.vector.tensor_tensor(
                out=wide[:, rt, cols],
                in0=qbytes[c][:, rt, cols].bitcast(FP8),
                in1=sc[:, cols],
                op=ALU.mult,
            )

        def new_group():
            grp = grpp.tile([P, NG, 4 * CH], BF16, name="grp", tag="grp", align_bytes=64)
            return grp

        def turn(rows, rt, grp):
            turn_half(rows, rt, grp, 0)
            turn_half(rows, rt, grp, 1)

        def turn_half(rows, rt, grp, half):
            words = rows[:, rt, :].bitcast(F32)
            gwords = grp[:].bitcast(F32)
            for gp in (half,):
                pt = ptp.tile([P, 2, 2, P], F32, name="pt", tag="pt")
                for gg in range(2):
                    g = 2 * gp + gg
                    for u in range(2):
                        nc.tensor.transpose(
                            pt[:, gg, u, :], words[:, 256 * g + u : 256 * (g + 1) : 2], ident[:]
                        )
                nc.scalar.copy(
                    out=gwords[:, 2 * gp : 2 * gp + 2, 256 * rt : 256 * (rt + 1)].rearrange(
                        "p g (r u) -> p g r u", u=2
                    ),
                    in_=pt[:].rearrange("p g u r -> p g r u"),
                )

        def quantize_half(grp, codes, scales, gp):
            gs = slice(2 * gp, 2 * gp + 2)
            nc.vector.quantize_mx(
                out=codes[:, gs, :].rearrange("p g n -> p (g n)").bitcast(FP8X4),
                scales=scales[:, gs, :].rearrange("p g n -> p (g n)"),
                in_=grp[:, gs, :].rearrange("p g n -> p (g n)"),
            )

        def quantize(grp, codes, scales):
            quantize_half(grp, codes, scales, 0)
            quantize_half(grp, codes, scales, 1)

        def new_codes():
            codes = codep.tile([P, NG, CH], U32, name="q_codes", tag="q_codes", align_bytes=64)
            scales = codep.tile([P, NG, CH], U8, name="q_scales", tag="q_scales", align_bytes=64)
            return codes, scales

        def multiply(codes, scales, pool, tag, tt):
            acc = pool.tile([P, CH], F32, name="acc", tag=tag)
            ts = slice(P * tt, P * (tt + 1))
            for g in range(NG):
                nc.tensor.matmul_mx(
                    out=acc[:],
                    lhsT=x_codes[:, g, ts].bitcast(FP8X4),
                    lhsT_scale=x_scales[:, g, ts],
                    rhs=codes[:, g, :].bitcast(FP8X4),
                    rhs_scale=scales[:, g, :],
                    start=(g == 0),
                    stop=(g == NG - 1),
                )
            return acc

        def project_normed(codes, scales, pool, tag):
            ss = statp.tile([P, 16], F32, name="ss", tag="ss")
            accs = []
            for tt in range(NT):
                acc = multiply(codes, scales, pool, tag, tt)
                for h in range(4):
                    nc.scalar.activation(
                        out=junk(),
                        in_=acc[:, D * h : D * (h + 1)],
                        func=ACT.Square,
                        accum_out=ss[:, 4 * tt + h : 4 * tt + h + 1],
                    )
                accs.append(acc)
            rms = statp.tile([P, 16], F32, name="rms", tag="rms")
            nc.scalar.activation(out=rms[:], in_=ss[:], func=ACT.Sqrt, scale=1.0 / D)
            return accs, plus_eps(rms)

        def project_bank(codes, scales, tt, ss):
            acc = multiply(codes, scales, accp, "acc", tt)
            for h in range(4):
                nc.scalar.activation(
                    out=junk(),
                    in_=acc[:, D * h : D * (h + 1)],
                    func=ACT.Square,
                    accum_out=ss[:, 4 * tt + h : 4 * tt + h + 1],
                )
            return acc

        def root(ss):
            rms = statp.tile([P, 16], F32, name="rms", tag="rms")
            nc.scalar.activation(out=rms[:], in_=ss[:], func=ACT.Sqrt, scale=1.0 / D)
            return plus_eps(rms)

        def products(accs, nm):
            prods = []
            for tt in range(NT):
                pair = prodp.tile([P, 2, CH], F32, name="pair", tag="pair")
                nc.vector.tensor_tensor(
                    out=pair[:].rearrange("p a (h d) -> p a h d", h=4),
                    in0=accs[tt][:].rearrange("p (h d) -> p h d", h=4).unsqueeze(1).to_broadcast([P, 2, 4, D]),
                    in1=tabs[nm][:, tt, :, :].unsqueeze(2).to_broadcast([P, 2, 4, D]),
                    op=ALU.mult,
                )
                prods.append(pair)
            return prods

        def plus_eps(rms):
            den = statp.tile([P, 16], F32, name="den", tag="den")
            nc.scalar.activation(out=den[:], in_=rms[:], func=ACT.Copy, bias=EPS)
            return den

        def add_eps(den):
            return den

        def invert(den):
            inv = statp.tile([P, 16], F32, name="inv", tag="inv")
            nc.vector.reciprocal(out=inv[:], in_=den[:])
            return inv

        spare = []
        taken = [0]

        def new_out():
            if taken[0] < len(spare):
                place = spare[taken[0]]
                taken[0] = taken[0] + 1
                return place
            tile = outp.tile([P, CH], F32, name="tsum", tag="tsum")
            return tile[:]

        def add_halves(engine, pair, tsum):
            engine.tensor_tensor(
                out=tsum.rearrange("p (h s j) -> p h s j", s=2, j=HALF),
                in0=pair[:, 0, :].rearrange("p (h s j) -> p h s j", s=2, j=HALF),
                in1=pair[:, 1, :].rearrange("p (h s j) -> p h s j", s=2, j=HALF)[:, :, ::-1, :],
                op=ALU.add,
            )

        def scale_store(tsum, inv, tt, dst, c, by_vector=False):
            for h in range(4):
                hs = slice(D * h, D * (h + 1))
                factor = inv[:, 4 * tt + h : 4 * tt + h + 1]
                if by_vector:
                    nc.vector.tensor_scalar_mul(out=tsum[:, hs], in0=tsum[:, hs], scalar1=factor)
                else:
                    nc.scalar.activation(out=tsum[:, hs], in_=tsum[:, hs], func=ACT.Copy, scale=factor)
            nc.sync.dma_start(out=dst[P * tt : P * (tt + 1), CH * c : CH * (c + 1)], in_=tsum)

        def bank(engine, prods, inv, tt, dst, c, by_vector=False):
            tsum = new_out()
            add_halves(engine, prods[tt], tsum)
            scale_store(tsum, inv, tt, dst, c, by_vector)

        def held_bank(prods, inv, dst, c):
            tsum = new_out()
            nc.vector.memset(tsum[:, 0:1], 0.0)
            add_halves(nc.gpsimd, prods[NT - 1], tsum)
            scale_store(tsum, inv, NT - 1, dst, c)

        grp_x = new_group()
        grp_q = new_group()
        wide = widep.tile([P, 4, C], BF16, name="wide", tag="wide")
        for first, last in ((0, 256), (256, 768), (768, 2048)):
            for rt in range(4):
                widen(0, rt, wide, slice(first, last))
                if last == C:
                    turn(x_raw, rt, grp_x)
                    turn(wide, rt, grp_q)
        tables_turn()
        v_raw = rawp.tile([P, 4, C], BF16, name="v_raw", tag="raw")
        load_rows(v_raw, Wv)

        wide_n = widep.tile([P, 4, C], BF16, name="wide", tag="wide")
        widen(1, 0, wide_n)
        widen(1, 1, wide_n)
        quantize(grp_x, x_codes, x_scales)
        grp_n = new_group()
        turn(wide_n, 0, grp_n)
        turn(wide_n, 1, grp_n)
        tables_multiply()
        codes, scales = new_codes()
        quantize(grp_q, codes, scales)
        accs, rms = project_normed(codes, scales, accp, "acc")
        widen(1, 2, wide_n)
        turn(wide_n, 2, grp_n)
        widen(1, 3, wide_n)
        turn(wide_n, 3, grp_n)
        wide_a = widep.tile([P, 4, C], BF16, name="wide", tag="wide")
        widen(2, 0, wide_a)

        held = None
        for c, side_raw, side_codes, side_scales in (
            (0, k_raw, k_codes, k_scales),
            (1, v_raw, None, None),
        ):
            grp_s = new_group()
            for rt in range(4):
                turn(side_raw, rt, grp_s)
            if held is not None:
                held_bank(*held)
            prods = products(accs, "q")
            den = add_eps(rms)
            codes, scales = new_codes()
            quantize_half(grp_n, codes, scales, 0)
            inv = invert(den)
            quantize_half(grp_n, codes, scales, 1)
            bank(nc.gpsimd, prods, inv, 0, o_q, c)
            bank(nc.gpsimd, prods, inv, 1, o_q, c)
            bank(nc.vector, prods, inv, 2, o_q, c)
            held = (prods, inv, o_q, c)
            ss = statp.tile([P, 16], F32, name="ss", tag="ss")
            grp_n = new_group()
            wide_n = wide_a
            turn(wide_n, 0, grp_n)
            accs = [project_bank(codes, scales, 0, ss), project_bank(codes, scales, 1, ss)]
            widen(c + 2, 1, wide_n)
            turn(wide_n, 1, grp_n)
            accs.append(project_bank(codes, scales, 2, ss))
            widen(c + 2, 2, wide_n)
            turn(wide_n, 2, grp_n)
            accs.append(project_bank(codes, scales, 3, ss))
            rms = root(ss)
            widen(c + 2, 3, wide_n)
            turn(wide_n, 3, grp_n)
            if side_codes is not None:
                quantize(grp_s, side_codes, side_scales)
                wide_a = widep.tile([P, 4, C], BF16, name="wide", tag="wide")
                widen(3, 0, wide_a)

        for i in range(2):
            big = widep.tile([P, 8, CH], F32, name="wide", tag="wide")
            spare.extend([big[:, j, :] for j in range(8)])
        accs_k, rms_k = project_normed(k_codes, k_scales, ptp, "pt")
        held_bank(*held)
        prods = products(accs, "q")
        den = add_eps(rms)
        codes, scales = new_codes()
        quantize_half(grp_n, codes, scales, 0)
        inv = invert(den)
        quantize_half(grp_n, codes, scales, 1)
        den_k = add_eps(rms_k)
        bank(nc.gpsimd, prods, inv, 0, o_q, 2)
        bank(nc.gpsimd, prods, inv, 1, o_q, 2)
        bank(nc.vector, prods, inv, 2, o_q, 2)
        held = (prods, inv, o_q, 2)
        accs, rms = project_normed(codes, scales, accp, "acc")
        quantize_half(grp_s, v_codes, v_scales, 0)
        inv_k = invert(den_k)
        quantize_half(grp_s, v_codes, v_scales, 1)

        held_bank(*held)
        prods = products(accs_k, "k")
        den = add_eps(rms)

        def finish_v(tt):
            acc = multiply(v_codes, v_scales, ptp, "pt", tt)
            res = new_out()
            nc.scalar.copy(out=res, in_=acc[:])
            nc.sync.dma_start(out=o_v[P * tt : P * (tt + 1), :], in_=res)

        finish_v(0)
        bank(nc.gpsimd, prods, inv_k, 0, o_k, 0)
        finish_v(1)
        bank(nc.gpsimd, prods, inv_k, 1, o_k, 0)
        finish_v(2)
        tsum = new_out()
        add_halves(nc.vector, prods[2], tsum)
        inv = invert(den)
        scale_store(tsum, inv_k, 2, o_k, 0)
        finish_v(3)

        held_bank(prods, inv_k, o_k, 0)
        prods = products(accs, "q")
        bank(nc.gpsimd, prods, inv, 0, o_q, 3)
        bank(nc.gpsimd, prods, inv, 1, o_q, 3)
        bank(nc.vector, prods, inv, 2, o_q, 3, by_vector=True)
        bank(nc.vector, prods, inv, 3, o_q, 3, by_vector=True)
